import numpy as np
import ml_dtypes


def mxq(x, axis, fmt="e4m3"):
    dtype, down = {"e4m3": (ml_dtypes.float8_e4m3fn, 7), "e5m2": (ml_dtypes.float8_e5m2, 14)}[fmt]
    v = np.moveaxis(np.asarray(x, np.float32).astype(ml_dtypes.bfloat16).astype(np.float64), axis, -1)
    blocks = v.reshape(v.shape[:-1] + (-1, 32))
    amax = np.abs(blocks).max(-1, keepdims=True)
    byte = np.maximum(np.where(amax > 0, np.frexp(amax)[1] - 1 + 127, 0) - down, 1)
    scale = np.exp2(byte - 127.0)
    codes = (blocks / scale).astype(np.float32).astype(dtype).astype(np.float64)
    return np.moveaxis((codes * scale).reshape(v.shape), -1, axis)


WIDE = False


def mx_kscale(k):
    if not WIDE:
        return np.ones(k)
    levels = np.array([10, -10, 5, -5, 0])
    if k % 512:
        return np.exp2(np.random.permutation(np.resize(levels, k // 32))).repeat(32)
    a = np.empty((k // 512, 16))
    for p in range(k // 512):
        a[p, :8] = np.random.permutation(np.resize(levels, 8))
        for g in range(8):
            far = levels[np.abs(levels - a[p, g]) >= 10]
            a[p, g + 8] = far[np.random.randint(len(far))]
    return np.exp2(a.ravel()).repeat(32)


BF16 = ml_dtypes.bfloat16


def bf(x):
    return np.asarray(x, np.float32).astype(BF16)


def f64(x):
    return np.asarray(x).astype(np.float64)


IN_C, OUT_C, N, ND = 512, 512, 4096, 2


def sigmoid(v):
    return 1.0 / (1.0 + np.exp(-v))


def setup_inputs():
    s, t = mx_kscale(IN_C), mx_kscale(OUT_C)
    rn = np.random.standard_normal
    return {"x": bf(rn((IN_C, N)) * s[:, None]),
            "h_prev_dim0": bf(rn((OUT_C, N)) * t[:, None]),
            "h_prev_dim1": bf(rn((OUT_C, N)) * t[:, None]),
            "ct0": bf(rn((OUT_C, N)) * 0.65),
            "ct1": bf(rn((OUT_C, N)) * 0.65),
            "w_io": bf(rn((OUT_C, IN_C)) * 0.7 / np.sqrt(IN_C) / s[None, :]),
            "w_ho": bf(rn((OUT_C, OUT_C)) * 0.7 / np.sqrt(OUT_C) / t[None, :]),
            "b_o": bf(rn((OUT_C, 1)) * 0.5),
            "weighted_sum": bf(0.4 + 0.5 * np.random.random(ND))}


def reference(x, h_prev_dim0, h_prev_dim1, ct0, ct1, w_io, w_ho, b_o, weighted_sum):
    xo = mxq(f64(w_io), 1, "e4m3") @ mxq(f64(x), 0, "e4m3")
    who = mxq(f64(w_ho), 1, "e4m3")
    ws = f64(weighted_sum)

    def hidden(h_prev, c):
        o = sigmoid(xo + (who @ mxq(f64(h_prev), 0, "e4m3")) + f64(b_o))
        return o * np.tanh(f64(c))

    ht0 = hidden(h_prev_dim0, ct0)
    ht1 = hidden(h_prev_dim1, ct1)
    return ht0 * ws[0] + ht1 * ws[1]

@@ -1,0 +1,273 @@
+from contextlib import ExitStack
+
+import concourse.mybir as mybir
+from concourse.masks import make_identity
+
+FLOPS = 3 * 2 * 512 * 512 * 4096
+
+F32 = mybir.dt.float32
+BF16 = mybir.dt.bfloat16
+U32 = mybir.dt.uint32
+U8 = mybir.dt.uint8
+I32 = mybir.dt.int32
+FP8X4 = mybir.dt.float8_e4m3fn_x4
+ACT = mybir.ActivationFunctionType
+ALU = mybir.AluOpType
+
+P = 128
+PACK = 4
+CH = 512
+MT = CH // P
+NPOS = 4096
+UNIT = 512
+N_UNITS = NPOS // UNIT
+CHUNKS = (1, 1, 2, 2, 2)
+SHARE = (512, 512, 512, 512, 512, 512, 512, 512)
+
+
+def tile_mdlstmcellweights_pb_t_kernel(
+    tc, x, h_prev_dim0, h_prev_dim1, ct0, ct1, w_io, w_ho, b_o, weighted_sum, out
+):
+    nc = tc.nc
+    with ExitStack() as ctx:
+        const = ctx.enter_context(tc.tile_pool(name="const", bufs=1))
+        rawp = ctx.enter_context(tc.tile_pool(name="rawp", bufs=2))
+        grpp = ctx.enter_context(tc.tile_pool(name="grpp", bufs=2))
+        codp = ctx.enter_context(tc.tile_pool(name="codp", bufs=3))
+        tp = ctx.enter_context(tc.tile_pool(name="tp", bufs=2))
+        psum = ctx.enter_context(tc.psum_pool(name="psum", bufs=8))
+
+        mov_views = [a.rearrange("(p t) n -> p t n", t=PACK) for a in (x, h_prev_dim0, h_prev_dim1)]
+        ct_views = [a.rearrange("(m p) n -> p m n", p=P) for a in (ct0, ct1)]
+        out_v = out.rearrange("(m p) n -> p m n", p=P)
+
+        chunk_of = []
+        chunk_start = []
+        for c, w in enumerate(CHUNKS):
+            chunk_start.append(len(chunk_of) * UNIT)
+            for i in range(w):
+                chunk_of.append((c, i))
+        n_chunks = len(CHUNKS)
+
+        def last_of_chunk(u):
+            return u + 1 >= N_UNITS or chunk_of[u + 1][0] != chunk_of[u][0]
+
+        raw_mov = {}
+        raw_ct = {}
+        grp = {}
+        codes = {}
+        tt = {}
+        oo = {}
+
+        def ldm(c, a):
+            w = CHUNKS[c] * UNIT
+            r = rawp.tile([P, PACK, w], BF16, name="rawm%d_%d" % (a, c), tag="rawm%d" % a)
+            nc.sync.dma_start(out=r[:], in_=mov_views[a][:, :, chunk_start[c]:chunk_start[c] + w])
+            raw_mov[(c, a)] = r
+
+        def ldc(c, d):
+            w = CHUNKS[c] * UNIT
+            r = rawp.tile([P, MT, w], BF16, name="rawc%d_%d" % (d, c), tag="rawc%d" % d)
+            nc.sync.dma_start(out=r[:], in_=ct_views[d][:, :, chunk_start[c]:chunk_start[c] + w])
+            raw_ct[(c, d)] = r
+
+        def rg(copy_fn, u, a, c0, c1):
+            if c1 <= c0:
+                return
+            if (u, a) not in grp:
+                grp[(u, a)] = grpp.tile([P, UNIT, PACK], BF16, name="grp%d_%d" % (a, u), tag="grp%d" % a, align_bytes=64)
+            c, s = chunk_of[u]
+            src = raw_mov[(c, a)][:, :, s * UNIT + c0:s * UNIT + c1]
+            copy_fn(
+                out=grp[(u, a)][:, c0:c1, :].rearrange("p (c i) t -> p c t i", i=4),
+                in_=src.rearrange("p t (c i) -> p c t i", i=4),
+            )
+
+        def rgv(u, a, c0=0, c1=UNIT):
+            rg(nc.vector.tensor_copy, u, a, c0, c1)
+
+        def rgs(u, a, c0, c1):
+            assert c0 == 0 and c1 == UNIT
+            grp[(u, a)] = grpp.tile([P, UNIT, PACK], BF16, name="grp%d_%d" % (a, u), tag="grp%d" % a, align_bytes=64)
+            c, s = chunk_of[u]
+            for hf in range(2):
+                bank = psum.tile([P, 2 * P * PACK], BF16, name="rgb%d_%d_%d" % (a, u, hf), tag="bank")
+                for qq in range(2):
+                    n0 = s * UNIT + (2 * hf + qq) * P
+                    nc.tensor.matmul(
+                        out=bank[:, qq * P * PACK:(qq + 1) * P * PACK].rearrange("p (n t) -> p t n", t=PACK),
+                        lhsT=ident[:], rhs=raw_mov[(c, a)][:, :, n0:n0 + P], start=True, stop=True,
+                    )
+                nc.scalar.copy(
+                    out=grp[(u, a)][:, 2 * hf * P:2 * (hf + 1) * P, :].rearrange("p n t -> p (n t)"), in_=bank[:]
+                )
+
+        def q(u, a):
+            cd = codp.tile([P, UNIT], U32, name="cod%d_%d" % (a, u), tag="cod%d" % a, align_bytes=64)
+            sc = codp.tile([P, UNIT], U8, name="scl%d_%d" % (a, u), tag="scl%d" % a, align_bytes=64)
+            nc.vector.quantize_mx(
+                out=cd[:].bitcast(FP8X4), scales=sc[:], in_=grp[(u, a)][:].rearrange("p n t -> p (n t)")
+            )
+            codes[(u, a)] = (cd, sc)
+
+        def tanh(u, d, m0=0, m1=MT):
+            if (u, d) not in tt:
+                tt[(u, d)] = tp.tile([P, MT, UNIT], F32, name="t%d_%d" % (d, u), tag="t%d" % d)
+            c, s = chunk_of[u]
+            nc.scalar.activation(
+                out=tt[(u, d)][:, m0:m1, :], in_=raw_ct[(c, d)][:, m0:m1, s * UNIT:(s + 1) * UNIT], func=ACT.Tanh
+            )
+
+        def mmsig(u, d, m):
+            if (u, d) not in oo:
+                oo[(u, d)] = op.tile([P, MT, UNIT], F32, name="o%d_%d" % (d, u), tag="o%d" % d, bufs=(3 if d == 0 else 2))
+            xc, xs = codes[(u, 0)]
+            hc, hs = codes[(u, 1 + d)]
+            acc = psum.tile([P, UNIT], F32, name="acc%d_%d_%d" % (u, d, m), tag="bank")
+            mc = slice(m * P, (m + 1) * P)
+            nc.tensor.matmul_mx(
+                out=acc[:], lhsT=w_codes[0][:, mc].bitcast(FP8X4), lhsT_scale=w_scales[0][:, mc],
+                rhs=xc[:].bitcast(FP8X4), rhs_scale=xs[:], start=True, stop=False,
+            )
+            nc.tensor.matmul_mx(
+                out=acc[:], lhsT=w_codes[1][:, mc].bitcast(FP8X4), lhsT_scale=w_scales[1][:, mc],
+                rhs=hc[:].bitcast(FP8X4), rhs_scale=hs[:], start=False, stop=True,
+            )
+            nc.scalar.activation(out=oo[(u, d)][:, m, :], in_=acc[:], func=ACT.Sigmoid, bias=b_sb[:, m:m + 1], scale=1.0)
+
+        def flat(t, m0, m1):
+            return t[:, m0:m1, :].rearrange("p m n -> p (m n)")
+
+        def prod(u, d, m0=0, m1=MT):
+            of = flat(oo[(u, d)], m0, m1)
+            nc.vector.scalar_tensor_tensor(
+                out=of, in0=of, scalar=ws_sb[:, d:d + 1], in1=flat(tt[(u, d)], m0, m1), op0=ALU.mult, op1=ALU.mult
+            )
+
+        def add(u, m0=0, m1=MT):
+            of = flat(oo[(u, 0)], m0, m1)
+            nc.vector.tensor_tensor(out=of, in0=of, in1=flat(oo[(u, 1)], m0, m1), op=ALU.add)
+
+        def st(u, m0=0, m1=MT):
+            nc.sync.dma_start(out=out_v[:, m0:m1, u * UNIT:(u + 1) * UNIT], in_=oo[(u, 0)][:, m0:m1, :])
+
+        warm = const.tile([P, 1], F32, name="warm")
+        nc.vector.memset(warm[:], 0.0)
+        nc.scalar.activation(out=warm[:], in_=warm[:], func=ACT.Sigmoid)
+        b_rows = const.tile([P, P], BF16, name="b_rows")
+        nc.vector.memset(b_rows[:].bitcast(I32), 0)
+        nc.scalar.dma_start(out=b_rows[0:MT, :], in_=b_o.rearrange("(m p) one -> m (p one)", p=P))
+        ws_bf = const.tile([P, 2], BF16, name="ws_bf")
+        nc.scalar.dma_start(out=ws_bf[:], in_=weighted_sum.partition_broadcast(P))
+        ident = const.tile([P, P], BF16, name="ident")
+        make_identity(nc, ident[:])
+
+        with tc.tile_pool(name="wtmp", bufs=1) as wtmp:
+            w_raws = []
+            for wi in range(2):
+                w_raws.append(wtmp.tile([P, MT, CH], BF16, name="w_raw%d" % wi))
+            nc.sync.dma_start(out=w_raws[0][:], in_=w_io.rearrange("(m p) k -> p m k", p=P))
+            ldc(0, 0)
+            ldm(0, 0)
+            nc.sync.dma_start(out=w_raws[1][:], in_=w_ho.rearrange("(m p) k -> p m k", p=P))
+            ldm(0, 1)
+            ldc(0, 1)
+            ldm(0, 2)
+            for a in range(3):
+                ldm(1, a)
+            for d in range(2):
+                ldc(1, d)
+            next_m = 2
+            next_c = 2
+
+            w_grps = []
+            for wi in range(2):
+                w_grp = wtmp.tile([P, MT, P, PACK], BF16, name="w_grp%d" % wi, align_bytes=64)
+                for m in range(MT):
+                    wt = psum.tile([P, PACK, P], BF16, name="wt%d_%d" % (wi, m), tag="bank")
+                    for t in range(PACK):
+                        nc.tensor.transpose(wt[:, t, :], w_raws[wi][:, m, t:CH:PACK], ident[:])
+                    nc.scalar.copy(out=w_grp[:, m], in_=wt[:].rearrange("p t o -> p o t"))
+                w_grps.append(w_grp)
+            b_ps = psum.tile([P, P], BF16, name="b_ps", tag="bank")
+            nc.tensor.transpose(b_ps[:], b_rows[:], ident[:])
+
+            w_codes = []
+            w_scales = []
+
+            def wq(wi):
+                wc = const.tile([P, MT * P], U32, name="w_codes%d" % wi, align_bytes=64)
+                wsc = const.tile([P, MT * P], U8, name="w_scales%d" % wi, align_bytes=64)
+                nc.vector.quantize_mx(
+                    out=wc[:].bitcast(FP8X4), scales=wsc[:], in_=w_grps[wi][:].rearrange("p m o t -> p (m o t)")
+                )
+                w_codes.append(wc)
+                w_scales.append(wsc)
+
+            wq(0)
+            rgv(0, 0)
+            wq(1)
+        op = ctx.enter_context(tc.tile_pool(name="op", bufs=2))
+        rgv(0, 1)
+        q(0, 0)
+        b_sb = const.tile([P, MT], F32, name="b_sb")
+        nc.vector.tensor_copy(out=b_sb[:], in_=b_ps[:, 0:MT])
+        ws_sb = const.tile([P, 2], F32, name="ws_sb")
+        nc.vector.tensor_copy(out=ws_sb[:], in_=ws_bf[:])
+        rgs(0, 2, UNIT - SHARE[0], UNIT)
+        rgv(0, 2, 0, UNIT - SHARE[0])
+        q(0, 1)
+        q(0, 2)
+        if last_of_chunk(0) and next_m < n_chunks:
+            for a in range(3):
+                ldm(next_m, a)
+            next_m += 1
+        tanh(0, 0)
+
+        for u in range(N_UNITS):
+            v = u + 1
+            has = v < N_UNITS
+            last = u == N_UNITS - 1
+            if has:
+                rgv(v, 0)
+                rgv(v, 1)
+                q(v, 0)
+                rgv(v, 2, 0, UNIT - SHARE[v])
+                q(v, 1)
+            if not last:
+                for m in range(MT):
+                    mmsig(u, 0, m)
+            if has:
+                rgs(v, 2, UNIT - SHARE[v], UNIT)
+            if not last:
+                tanh(u, 1)
+                if last_of_chunk(u) and next_c < n_chunks:
+                    for d in range(2):
+                        ldc(next_c, d)
+                    next_c += 1
+            if not last:
+                prod(u, 0)
+            if has:
+                q(v, 2)
+                if last_of_chunk(v) and next_m < n_chunks:
+                    for a in range(3):
+                        ldm(next_m, a)
+                    next_m += 1
+            if not last:
+                for m in range(MT):
+                    mmsig(u, 1, m)
+                if v < N_UNITS - 1:
+                    tanh(v, 0)
+                prod(u, 1)
+                add(u)
+                st(u)
+            else:
+                for m in range(MT):
+                    tanh(u, 0, m, m + 1)
+                    mmsig(u, 0, m)
+                    prod(u, 0, m, m + 1)
+                    tanh(u, 1, m, m + 1)
+                    mmsig(u, 1, m)
+                    prod(u, 1, m, m + 1)
+                    add(u, m, m + 1)
+                    st(u, m, m + 1)

@@ -9,7 +9,6 @@ F32 = mybir.dt.float32
 BF16 = mybir.dt.bfloat16
 U32 = mybir.dt.uint32
 U8 = mybir.dt.uint8
-I32 = mybir.dt.int32
 FP8X4 = mybir.dt.float8_e4m3fn_x4
 ACT = mybir.ActivationFunctionType
 ALU = mybir.AluOpType
@@ -22,7 +21,6 @@ NPOS = 4096
 UNIT = 512
 N_UNITS = NPOS // UNIT
 CHUNKS = (1, 1, 2, 2, 2)
-SHARE = (512, 512, 512, 512, 512, 512, 512, 512)
 
 
 def tile_mdlstmcellweights_pb_t_kernel(
@@ -33,13 +31,14 @@ def tile_mdlstmcellweights_pb_t_kernel(
         const = ctx.enter_context(tc.tile_pool(name="const", bufs=1))
         rawp = ctx.enter_context(tc.tile_pool(name="rawp", bufs=2))
         grpp = ctx.enter_context(tc.tile_pool(name="grpp", bufs=2))
-        codp = ctx.enter_context(tc.tile_pool(name="codp", bufs=3))
-        tp = ctx.enter_context(tc.tile_pool(name="tp", bufs=2))
+        codp = ctx.enter_context(tc.tile_pool(name="codp", bufs=2))
+        tp = ctx.enter_context(tc.tile_pool(name="tp", bufs=3))
         psum = ctx.enter_context(tc.psum_pool(name="psum", bufs=8))
+        ctx.enter_context(tc.manual_schedule())
 
         mov_views = [a.rearrange("(p t) n -> p t n", t=PACK) for a in (x, h_prev_dim0, h_prev_dim1)]
-        ct_views = [a.rearrange("(m p) n -> p m n", p=P) for a in (ct0, ct1)]
-        out_v = out.rearrange("(m p) n -> p m n", p=P)
+        ct_views = [a.rearrange("(p m) n -> p m n", m=MT) for a in (ct0, ct1)]
+        out_v = out.rearrange("(p m) n -> p m n", m=MT)
 
         chunk_of = []
         chunk_start = []
@@ -60,35 +59,36 @@ def tile_mdlstmcellweights_pb_t_kernel(
         oo = {}
 
         def ldm(c, a):
+            if c >= n_chunks:
+                return
             w = CHUNKS[c] * UNIT
             r = rawp.tile([P, PACK, w], BF16, name="rawm%d_%d" % (a, c), tag="rawm%d" % a)
             nc.sync.dma_start(out=r[:], in_=mov_views[a][:, :, chunk_start[c]:chunk_start[c] + w])
             raw_mov[(c, a)] = r
 
         def ldc(c, d):
+            if c >= n_chunks:
+                return
             w = CHUNKS[c] * UNIT
             r = rawp.tile([P, MT, w], BF16, name="rawc%d_%d" % (d, c), tag="rawc%d" % d)
             nc.sync.dma_start(out=r[:], in_=ct_views[d][:, :, chunk_start[c]:chunk_start[c] + w])
             raw_ct[(c, d)] = r
 
-        def rg(copy_fn, u, a, c0, c1):
-            if c1 <= c0:
-                return
-            if (u, a) not in grp:
-                grp[(u, a)] = grpp.tile([P, UNIT, PACK], BF16, name="grp%d_%d" % (a, u), tag="grp%d" % a, align_bytes=64)
+        def new_grp(u, a):
+            grp[(u, a)] = grpp.tile([P, UNIT, PACK], BF16, name="grp%d_%d" % (a, u), tag="grp%d" % a, align_bytes=64)
+            return grp[(u, a)]
+
+        def rgv(u, a):
+            g = new_grp(u, a)
             c, s = chunk_of[u]
-            src = raw_mov[(c, a)][:, :, s * UNIT + c0:s * UNIT + c1]
-            copy_fn(
-                out=grp[(u, a)][:, c0:c1, :].rearrange("p (c i) t -> p c t i", i=4),
-                in_=src.rearrange("p t (c i) -> p c t i", i=4),
+            nc.vector.tensor_copy(
+                out=g[:].rearrange("p (c i) t -> p c t i", i=4),
+                in_=raw_mov[(c, a)][:, :, s * UNIT:(s + 1) * UNIT].rearrange("p t (c i) -> p c t i", i=4),
             )
 
-        def rgv(u, a, c0=0, c1=UNIT):
-            rg(nc.vector.tensor_copy, u, a, c0, c1)
+        rgb = {}
 
-        def rgs(u, a, c0, c1):
-            assert c0 == 0 and c1 == UNIT
-            grp[(u, a)] = grpp.tile([P, UNIT, PACK], BF16, name="grp%d_%d" % (a, u), tag="grp%d" % a, align_bytes=64)
+        def rgp(u, a):
             c, s = chunk_of[u]
             for hf in range(2):
                 bank = psum.tile([P, 2 * P * PACK], BF16, name="rgb%d_%d_%d" % (a, u, hf), tag="bank")
@@ -98,8 +98,13 @@ def tile_mdlstmcellweights_pb_t_kernel(
                         out=bank[:, qq * P * PACK:(qq + 1) * P * PACK].rearrange("p (n t) -> p t n", t=PACK),
                         lhsT=ident[:], rhs=raw_mov[(c, a)][:, :, n0:n0 + P], start=True, stop=True,
                     )
+                rgb[(u, a, hf)] = bank
+
+        def rgc(u, a):
+            g = new_grp(u, a)
+            for hf in range(2):
                 nc.scalar.copy(
-                    out=grp[(u, a)][:, 2 * hf * P:2 * (hf + 1) * P, :].rearrange("p n t -> p (n t)"), in_=bank[:]
+                    out=g[:, 2 * hf * P:2 * (hf + 1) * P, :].rearrange("p n t -> p (n t)"), in_=rgb[(u, a, hf)][:]
                 )
 
         def q(u, a):
@@ -118,9 +123,9 @@ def tile_mdlstmcellweights_pb_t_kernel(
                 out=tt[(u, d)][:, m0:m1, :], in_=raw_ct[(c, d)][:, m0:m1, s * UNIT:(s + 1) * UNIT], func=ACT.Tanh
             )
 
-        def mmsig(u, d, m):
-            if (u, d) not in oo:
-                oo[(u, d)] = op.tile([P, MT, UNIT], F32, name="o%d_%d" % (d, u), tag="o%d" % d, bufs=(3 if d == 0 else 2))
+        accs = {}
+
+        def mm(u, d, m):
             xc, xs = codes[(u, 0)]
             hc, hs = codes[(u, 1 + d)]
             acc = psum.tile([P, UNIT], F32, name="acc%d_%d_%d" % (u, d, m), tag="bank")
@@ -133,7 +138,20 @@ def tile_mdlstmcellweights_pb_t_kernel(
                 out=acc[:], lhsT=w_codes[1][:, mc].bitcast(FP8X4), lhsT_scale=w_scales[1][:, mc],
                 rhs=hc[:].bitcast(FP8X4), rhs_scale=hs[:], start=False, stop=True,
             )
-            nc.scalar.activation(out=oo[(u, d)][:, m, :], in_=acc[:], func=ACT.Sigmoid, bias=b_sb[:, m:m + 1], scale=1.0)
+            accs[(u, d, m)] = acc
+
+        def sig(u, d, m):
+            if (u, d) not in oo:
+                oo[(u, d)] = op.tile([P, MT, UNIT], F32, name="o%d_%d" % (d, u), tag="o%d" % d, bufs=(3 if d == 0 else 2))
+            nc.scalar.activation(
+                out=oo[(u, d)][:, m, :], in_=accs[(u, d, m)][:], func=ACT.Sigmoid, bias=b_sb[:, m:m + 1], scale=1.0
+            )
+
+        def gates(u, d):
+            for m in range(MT):
+                mm(u, d, m)
+            for m in range(MT):
+                sig(u, d, m)
 
         def flat(t, m0, m1):
             return t[:, m0:m1, :].rearrange("p m n -> p (m n)")
@@ -154,120 +172,117 @@ def tile_mdlstmcellweights_pb_t_kernel(
         warm = const.tile([P, 1], F32, name="warm")
         nc.vector.memset(warm[:], 0.0)
         nc.scalar.activation(out=warm[:], in_=warm[:], func=ACT.Sigmoid)
-        b_rows = const.tile([P, P], BF16, name="b_rows")
-        nc.vector.memset(b_rows[:].bitcast(I32), 0)
-        nc.scalar.dma_start(out=b_rows[0:MT, :], in_=b_o.rearrange("(m p) one -> m (p one)", p=P))
-        ws_bf = const.tile([P, 2], BF16, name="ws_bf")
-        nc.scalar.dma_start(out=ws_bf[:], in_=weighted_sum.partition_broadcast(P))
+        ident_f = const.tile([P, P], F32, name="ident_f")
+        make_identity(nc, ident_f[:])
         ident = const.tile([P, P], BF16, name="ident")
-        make_identity(nc, ident[:])
+        nc.vector.tensor_copy(out=ident[:], in_=ident_f[:])
+        b_sb = const.tile([P, MT], BF16, name="b_sb")
+        ws_sb = const.tile([P, 2], BF16, name="ws_sb")
 
         with tc.tile_pool(name="wtmp", bufs=1) as wtmp:
-            w_raws = []
-            for wi in range(2):
-                w_raws.append(wtmp.tile([P, MT, CH], BF16, name="w_raw%d" % wi))
-            nc.sync.dma_start(out=w_raws[0][:], in_=w_io.rearrange("(m p) k -> p m k", p=P))
-            ldc(0, 0)
+            w_raws = [wtmp.tile([P, MT, CH], BF16, name="w_raw%d" % wi) for wi in range(2)]
+            w_grps = [wtmp.tile([P, MT * P * PACK], BF16, name="w_grp%d" % wi, align_bytes=64) for wi in range(2)]
+
+            def ldw(wi):
+                nc.sync.dma_start(out=w_raws[wi][:], in_=(w_io, w_ho)[wi].rearrange("(p m) k -> p m k", m=MT))
+
             ldm(0, 0)
-            nc.sync.dma_start(out=w_raws[1][:], in_=w_ho.rearrange("(m p) k -> p m k", p=P))
+            ldc(0, 0)
             ldm(0, 1)
-            ldc(0, 1)
+            ldw(0)
             ldm(0, 2)
+            ldw(1)
+            nc.sync.dma_start(out=b_sb[:], in_=b_o.rearrange("(p m) one -> p (m one)", m=MT))
+            nc.sync.dma_start(out=ws_sb[:], in_=weighted_sum.partition_broadcast(P))
+            ldc(0, 1)
             for a in range(3):
                 ldm(1, a)
             for d in range(2):
                 ldc(1, d)
-            next_m = 2
-            next_c = 2
 
-            w_grps = []
-            for wi in range(2):
-                w_grp = wtmp.tile([P, MT, P, PACK], BF16, name="w_grp%d" % wi, align_bytes=64)
-                for m in range(MT):
-                    wt = psum.tile([P, PACK, P], BF16, name="wt%d_%d" % (wi, m), tag="bank")
-                    for t in range(PACK):
-                        nc.tensor.transpose(wt[:, t, :], w_raws[wi][:, m, t:CH:PACK], ident[:])
-                    nc.scalar.copy(out=w_grp[:, m], in_=wt[:].rearrange("p t o -> p o t"))
-                w_grps.append(w_grp)
-            b_ps = psum.tile([P, P], BF16, name="b_ps", tag="bank")
-            nc.tensor.transpose(b_ps[:], b_rows[:], ident[:])
+            w_codes = [const.tile([P, MT * P], U32, name="w_codes%d" % wi, align_bytes=64) for wi in range(2)]
+            w_scales = [const.tile([P, MT * P], U8, name="w_scales%d" % wi, align_bytes=64) for wi in range(2)]
 
-            w_codes = []
-            w_scales = []
+            def w_turn(wi):
+                words = w_raws[wi][:].rearrange("p m k -> p (m k)").bitcast(F32)
+                half = CH // 2
+                for mp in range(2):
+                    wt = psum.tile([P, 2, 2, P], F32, name="wt%d_%d" % (wi, mp), tag="bank")
+                    for j in range(2):
+                        m = 2 * mp + j
+                        for e in range(2):
+                            nc.tensor.transpose(wt[:, j, e, :], words[:, m * half + e:(m + 1) * half:2], ident_f[:])
+                    nc.scalar.copy(
+                        out=w_grps[wi][:].bitcast(F32)[:, mp * 4 * P:(mp + 1) * 4 * P].rearrange("p (j o e) -> p j o e", j=2, e=2),
+                        in_=wt[:].rearrange("p j e o -> p j o e"),
+                    )
 
             def wq(wi):
-                wc = const.tile([P, MT * P], U32, name="w_codes%d" % wi, align_bytes=64)
-                wsc = const.tile([P, MT * P], U8, name="w_scales%d" % wi, align_bytes=64)
                 nc.vector.quantize_mx(
-                    out=wc[:].bitcast(FP8X4), scales=wsc[:], in_=w_grps[wi][:].rearrange("p m o t -> p (m o t)")
+                    out=w_codes[wi][:].bitcast(FP8X4), scales=w_scales[wi][:], in_=w_grps[wi][:]
                 )
-                w_codes.append(wc)
-                w_scales.append(wsc)
 
-            wq(0)
             rgv(0, 0)
+            tanh(0, 0)
+            rgv(0, 1)
+            w_turn(0)
+            q(0, 0)
+            rgv(0, 2)
+            w_turn(1)
+            q(0, 1)
+            wq(0)
+            q(0, 2)
             wq(1)
-        op = ctx.enter_context(tc.tile_pool(name="op", bufs=2))
-        rgv(0, 1)
-        q(0, 0)
-        b_sb = const.tile([P, MT], F32, name="b_sb")
-        nc.vector.tensor_copy(out=b_sb[:], in_=b_ps[:, 0:MT])
-        ws_sb = const.tile([P, 2], F32, name="ws_sb")
-        nc.vector.tensor_copy(out=ws_sb[:], in_=ws_bf[:])
-        rgs(0, 2, UNIT - SHARE[0], UNIT)
-        rgv(0, 2, 0, UNIT - SHARE[0])
-        q(0, 1)
-        q(0, 2)
-        if last_of_chunk(0) and next_m < n_chunks:
             for a in range(3):
-                ldm(next_m, a)
-            next_m += 1
-        tanh(0, 0)
+                ldm(2, a)
+        op = ctx.enter_context(tc.tile_pool(name="op", bufs=2))
 
-        for u in range(N_UNITS):
-            v = u + 1
-            has = v < N_UNITS
-            last = u == N_UNITS - 1
-            if has:
+        for i in range(-1, N_UNITS):
+            g = i + 1
+            v = i + 2
+            if v < N_UNITS:
+                if i >= 0:
+                    prod(i, 0)
+                if i >= 0:
+                    tanh(g, 0)
                 rgv(v, 0)
+                gates(g, 0)
+                if i >= 0:
+                    prod(i, 1)
                 rgv(v, 1)
+                rgp(v, 2)
+                rgc(v, 2)
+                tanh(g, 1)
+                if i >= 0:
+                    add(i)
                 q(v, 0)
-                rgv(v, 2, 0, UNIT - SHARE[v])
                 q(v, 1)
-            if not last:
-                for m in range(MT):
-                    mmsig(u, 0, m)
-            if has:
-                rgs(v, 2, UNIT - SHARE[v], UNIT)
-            if not last:
-                tanh(u, 1)
-                if last_of_chunk(u) and next_c < n_chunks:
-                    for d in range(2):
-                        ldc(next_c, d)
-                    next_c += 1
-            if not last:
-                prod(u, 0)
-            if has:
+                gates(g, 1)
                 q(v, 2)
-                if last_of_chunk(v) and next_m < n_chunks:
+                if last_of_chunk(v):
                     for a in range(3):
-                        ldm(next_m, a)
-                    next_m += 1
-            if not last:
+                        ldm(chunk_of[v][0] + 2, a)
+                if i >= 0:
+                    st(i)
+                if last_of_chunk(g):
+                    for d in range(2):
+                        ldc(chunk_of[g][0] + 2, d)
+            elif g < N_UNITS:
+                prod(i, 0)
+                tanh(g, 0)
+                gates(g, 0)
+                prod(i, 1)
                 for m in range(MT):
-                    mmsig(u, 1, m)
-                if v < N_UNITS - 1:
-                    tanh(v, 0)
-                prod(u, 1)
-                add(u)
-                st(u)
+                    mm(g, 1, m)
+                for m in range(MT):
+                    tanh(g, 1, m, m + 1)
+                    sig(g, 1, m)
+                add(i)
+                st(i)
             else:
+                prod(i, 0, 0, 2)
+                prod(i, 0, 2, 4)
                 for m in range(MT):
-                    tanh(u, 0, m, m + 1)
-                    mmsig(u, 0, m)
-                    prod(u, 0, m, m + 1)
-                    tanh(u, 1, m, m + 1)
-                    mmsig(u, 1, m)
-                    prod(u, 1, m, m + 1)
-                    add(u, m, m + 1)
-                    st(u, m, m + 1)
+                    prod(i, 1, m, m + 1)
+                    add(i, m, m + 1)
+                    st(i, m, m + 1)

@@ -21,6 +21,7 @@ NPOS = 4096
 UNIT = 512
 N_UNITS = NPOS // UNIT
 CHUNKS = (1, 1, 2, 2, 2)
+BY_TENSOR = frozenset([(u, 2) for u in range(1, N_UNITS)] + [(3, 1), (5, 1)])
 
 
 def tile_mdlstmcellweights_pb_t_kernel(
@@ -187,18 +188,24 @@ def tile_mdlstmcellweights_pb_t_kernel(
                 nc.sync.dma_start(out=w_raws[wi][:], in_=(w_io, w_ho)[wi].rearrange("(p m) k -> p m k", m=MT))
 
             ldm(0, 0)
-            ldc(0, 0)
             ldm(0, 1)
             ldw(0)
-            ldm(0, 2)
             ldw(1)
+            ldc(0, 0)
             nc.sync.dma_start(out=b_sb[:], in_=b_o.rearrange("(p m) one -> p (m one)", m=MT))
             nc.sync.dma_start(out=ws_sb[:], in_=weighted_sum.partition_broadcast(P))
+            ldm(0, 2)
             ldc(0, 1)
-            for a in range(3):
-                ldm(1, a)
-            for d in range(2):
-                ldc(1, d)
+            ldm(1, 0)
+            ldm(1, 1)
+            ldm(1, 2)
+            ldc(1, 0)
+            ldc(1, 1)
+            ldm(2, 0)
+            ldm(2, 1)
+            ldm(2, 2)
+            ldc(2, 0)
+            ldc(2, 1)
 
             w_codes = [const.tile([P, MT * P], U32, name="w_codes%d" % wi, align_bytes=64) for wi in range(2)]
             w_scales = [const.tile([P, MT * P], U8, name="w_scales%d" % wi, align_bytes=64) for wi in range(2)]
@@ -223,66 +230,66 @@ def tile_mdlstmcellweights_pb_t_kernel(
                 )
 
             rgv(0, 0)
-            tanh(0, 0)
             rgv(0, 1)
             w_turn(0)
             q(0, 0)
-            rgv(0, 2)
-            w_turn(1)
             q(0, 1)
+            w_turn(1)
             wq(0)
-            q(0, 2)
             wq(1)
-            for a in range(3):
-                ldm(2, a)
+            rgv(0, 2)
+            tanh(0, 0)
+            q(0, 2)
         op = ctx.enter_context(tc.tile_pool(name="op", bufs=2))
 
-        for i in range(-1, N_UNITS):
-            g = i + 1
-            v = i + 2
-            if v < N_UNITS:
-                if i >= 0:
-                    prod(i, 0)
-                if i >= 0:
-                    tanh(g, 0)
-                rgv(v, 0)
-                gates(g, 0)
-                if i >= 0:
-                    prod(i, 1)
+        def turn_raw(v):
+            for a in range(3):
+                if (v, a) in BY_TENSOR:
+                    rgp(v, a)
+                    rgc(v, a)
+
+
+        for m in range(MT):
+            mm(0, 0, m)
+            sig(0, 0, m)
+        gates(0, 1)
+        tanh(0, 1)
+        rgv(1, 0)
+        for i in range(N_UNITS - 1):
+            v = i + 1
+            turn_raw(v)
+            if (v, 1) not in BY_TENSOR:
                 rgv(v, 1)
-                rgp(v, 2)
-                rgc(v, 2)
-                tanh(g, 1)
-                if i >= 0:
-                    add(i)
-                q(v, 0)
-                q(v, 1)
-                gates(g, 1)
-                q(v, 2)
-                if last_of_chunk(v):
-                    for a in range(3):
-                        ldm(chunk_of[v][0] + 2, a)
-                if i >= 0:
-                    st(i)
-                if last_of_chunk(g):
-                    for d in range(2):
-                        ldc(chunk_of[g][0] + 2, d)
-            elif g < N_UNITS:
-                prod(i, 0)
-                tanh(g, 0)
-                gates(g, 0)
-                prod(i, 1)
-                for m in range(MT):
-                    mm(g, 1, m)
-                for m in range(MT):
-                    tanh(g, 1, m, m + 1)
-                    sig(g, 1, m)
+            q(v, 0)
+            prod(i, 0)
+            q(v, 1)
+            tanh(v, 0)
+            gates(v, 0)
+            prod(i, 1)
+            q(v, 2)
+            tanh(v, 1)
+            if v + 1 < N_UNITS:
+                rgv(v + 1, 0)
+            if last_of_chunk(v):
+                for a in range(3):
+                    ldm(chunk_of[v][0] + 2, a)
+            if v + 1 < N_UNITS:
+                gates(v, 1)
                 add(i)
                 st(i)
-            else:
-                prod(i, 0, 0, 2)
-                prod(i, 0, 2, 4)
-                for m in range(MT):
-                    prod(i, 1, m, m + 1)
-                    add(i, m, m + 1)
-                    st(i, m, m + 1)
+            if i > 0 and last_of_chunk(i):
+                for d in range(2):
+                    ldc(chunk_of[i][0] + 2, d)
+        g = N_UNITS - 1
+        for m in range(MT):
+            mm(g, 1, m)
+            sig(g, 1, m)
+        prod(g, 0, 0, 1)
+        add(g - 1)
+        st(g - 1)
+        for m in range(MT):
+            prod(g, 1, m, m + 1)
+            if m + 1 < MT:
+                prod(g, 0, m + 1, m + 2)
+            add(g, m, m + 1)
+            st(g, m, m + 1)

@@ -18,10 +18,15 @@ PACK = 4
 CH = 512
 MT = CH // P
 NPOS = 4096
-UNIT = 512
-N_UNITS = NPOS // UNIT
-CHUNKS = (1, 1, 2, 2, 2)
-BY_TENSOR = frozenset([(u, 2) for u in range(1, N_UNITS)] + [(3, 1), (5, 1)])
+UNITS = 8 * (512,)
+N_UNITS = len(UNITS)
+LOADS = (512, 512, 512, 512, 1024, 1024)
+def by_tensor(u, a):
+    if u == 0:
+        return 0
+    if u == 1:
+        return (0, 0, UNITS[u])[a]
+    return (0, 128, UNITS[u])[a]
 
 
 def tile_mdlstmcellweights_pb_t_kernel(
@@ -37,99 +42,102 @@ def tile_mdlstmcellweights_pb_t_kernel(
         psum = ctx.enter_context(tc.psum_pool(name="psum", bufs=8))
         ctx.enter_context(tc.manual_schedule())
 
-        mov_views = [a.rearrange("(p t) n -> p t n", t=PACK) for a in (x, h_prev_dim0, h_prev_dim1)]
-        ct_views = [a.rearrange("(p m) n -> p m n", m=MT) for a in (ct0, ct1)]
+        names = ("x", "h0", "h1", "c0", "c1")
+        views = {}
+        for nm, a in zip(names, (x, h_prev_dim0, h_prev_dim1, ct0, ct1)):
+            views[nm] = a.rearrange("(p t) n -> p t n", t=PACK)
         out_v = out.rearrange("(p m) n -> p m n", m=MT)
 
-        chunk_of = []
-        chunk_start = []
-        for c, w in enumerate(CHUNKS):
-            chunk_start.append(len(chunk_of) * UNIT)
-            for i in range(w):
-                chunk_of.append((c, i))
-        n_chunks = len(CHUNKS)
+        start = [sum(UNITS[:u]) for u in range(N_UNITS + 1)]
+        where = {}
+        last_unit = {}
+        first = {}
+        for nm in names:
+            at = 0
+            for c, w in enumerate(LOADS):
+                first[(nm, c)] = at
+                for u in range(N_UNITS):
+                    if at <= start[u] and start[u + 1] <= at + w:
+                        where[(nm, u)] = (c, start[u] - at)
+                        last_unit[(nm, c)] = u
+                at += w
 
-        def last_of_chunk(u):
-            return u + 1 >= N_UNITS or chunk_of[u + 1][0] != chunk_of[u][0]
-
-        raw_mov = {}
-        raw_ct = {}
+        raw = {}
         grp = {}
         codes = {}
         tt = {}
         oo = {}
+        bank_of = {}
+        accs = {}
 
-        def ldm(c, a):
-            if c >= n_chunks:
+        def ld(nm, c):
+            if c >= len(LOADS):
                 return
-            w = CHUNKS[c] * UNIT
-            r = rawp.tile([P, PACK, w], BF16, name="rawm%d_%d" % (a, c), tag="rawm%d" % a)
-            nc.sync.dma_start(out=r[:], in_=mov_views[a][:, :, chunk_start[c]:chunk_start[c] + w])
-            raw_mov[(c, a)] = r
+            w = LOADS[c]
+            r = rawp.tile([P, PACK, w], BF16, name="raw_%s_%d" % (nm, c), tag="raw_" + nm)
+            nc.sync.dma_start(out=r[:], in_=views[nm][:, :, first[(nm, c)]:first[(nm, c)] + w])
+            raw[(nm, c)] = r
 
-        def ldc(c, d):
-            if c >= n_chunks:
-                return
-            w = CHUNKS[c] * UNIT
-            r = rawp.tile([P, MT, w], BF16, name="rawc%d_%d" % (d, c), tag="rawc%d" % d)
-            nc.sync.dma_start(out=r[:], in_=ct_views[d][:, :, chunk_start[c]:chunk_start[c] + w])
-            raw_ct[(c, d)] = r
+        def reload(nm, u):
+            c = where[(nm, u)][0]
+            if last_unit[(nm, c)] == u:
+                ld(nm, c + 2)
 
-        def new_grp(u, a):
-            grp[(u, a)] = grpp.tile([P, UNIT, PACK], BF16, name="grp%d_%d" % (a, u), tag="grp%d" % a, align_bytes=64)
+        def raw_cols(nm, u, c0, c1):
+            c, s = where[(nm, u)]
+            return raw[(nm, c)][:, :, s + c0:s + c1]
+
+        def grouped(u, a):
+            if (u, a) not in grp:
+                grp[(u, a)] = grpp.tile([P, UNITS[u], PACK], BF16, name="grp%d_%d" % (a, u), tag="grp%d" % a, align_bytes=64)
             return grp[(u, a)]
 
-        def rgv(u, a):
-            g = new_grp(u, a)
-            c, s = chunk_of[u]
+        def rgv(u, a, c0=None, c1=None):
+            c0 = by_tensor(u, a) if c0 is None else c0
+            c1 = UNITS[u] if c1 is None else c1
+            if c0 == c1:
+                return
             nc.vector.tensor_copy(
-                out=g[:].rearrange("p (c i) t -> p c t i", i=4),
-                in_=raw_mov[(c, a)][:, :, s * UNIT:(s + 1) * UNIT].rearrange("p t (c i) -> p c t i", i=4),
+                out=grouped(u, a)[:, c0:c1, :].rearrange("p (c i) t -> p c t i", i=4),
+                in_=raw_cols(names[a], u, c0, c1).rearrange("p t (c i) -> p c t i", i=4),
             )
 
-        rgb = {}
+        def banks(u, a):
+            return [(b0, min(b0 + 2 * P, by_tensor(u, a))) for b0 in range(0, by_tensor(u, a), 2 * P)]
 
         def rgp(u, a):
-            c, s = chunk_of[u]
-            for hf in range(2):
-                bank = psum.tile([P, 2 * P * PACK], BF16, name="rgb%d_%d_%d" % (a, u, hf), tag="bank")
-                for qq in range(2):
-                    n0 = s * UNIT + (2 * hf + qq) * P
+            for b0, b1 in banks(u, a):
+                bank = psum.tile([P, (b1 - b0) * PACK], BF16, name="rgb%d_%d_%d" % (a, u, b0), tag="bank")
+                for n0 in range(b0, b1, P):
                     nc.tensor.matmul(
-                        out=bank[:, qq * P * PACK:(qq + 1) * P * PACK].rearrange("p (n t) -> p t n", t=PACK),
-                        lhsT=ident[:], rhs=raw_mov[(c, a)][:, :, n0:n0 + P], start=True, stop=True,
+                        out=bank[:, (n0 - b0) * PACK:(n0 - b0 + P) * PACK].rearrange("p (n t) -> p t n", t=PACK),
+                        lhsT=ident[:], rhs=raw_cols(names[a], u, n0, n0 + P), start=True, stop=True,
                     )
-                rgb[(u, a, hf)] = bank
+                bank_of[(u, a, b0)] = bank
 
         def rgc(u, a):
-            g = new_grp(u, a)
-            for hf in range(2):
+            for b0, b1 in banks(u, a):
                 nc.scalar.copy(
-                    out=g[:, 2 * hf * P:2 * (hf + 1) * P, :].rearrange("p n t -> p (n t)"), in_=rgb[(u, a, hf)][:]
+                    out=grouped(u, a)[:, b0:b1, :].rearrange("p n t -> p (n t)"), in_=bank_of[(u, a, b0)][:]
                 )
 
         def q(u, a):
-            cd = codp.tile([P, UNIT], U32, name="cod%d_%d" % (a, u), tag="cod%d" % a, align_bytes=64)
-            sc = codp.tile([P, UNIT], U8, name="scl%d_%d" % (a, u), tag="scl%d" % a, align_bytes=64)
+            w = UNITS[u]
+            cd = codp.tile([P, w], U32, name="cod%d_%d" % (a, u), tag="cod%d" % a, align_bytes=64)
+            sc = codp.tile([P, w], U8, name="scl%d_%d" % (a, u), tag="scl%d" % a, align_bytes=64)
             nc.vector.quantize_mx(
                 out=cd[:].bitcast(FP8X4), scales=sc[:], in_=grp[(u, a)][:].rearrange("p n t -> p (n t)")
             )
             codes[(u, a)] = (cd, sc)
 
-        def tanh(u, d, m0=0, m1=MT):
-            if (u, d) not in tt:
-                tt[(u, d)] = tp.tile([P, MT, UNIT], F32, name="t%d_%d" % (d, u), tag="t%d" % d)
-            c, s = chunk_of[u]
-            nc.scalar.activation(
-                out=tt[(u, d)][:, m0:m1, :], in_=raw_ct[(c, d)][:, m0:m1, s * UNIT:(s + 1) * UNIT], func=ACT.Tanh
-            )
-
-        accs = {}
+        def tanh(u, d):
+            tt[(u, d)] = tp.tile([P, MT, UNITS[u]], F32, name="t%d_%d" % (d, u), tag="t%d" % d)
+            nc.scalar.activation(out=tt[(u, d)][:], in_=raw_cols(names[3 + d], u, 0, UNITS[u]), func=ACT.Tanh)
 
         def mm(u, d, m):
             xc, xs = codes[(u, 0)]
             hc, hs = codes[(u, 1 + d)]
-            acc = psum.tile([P, UNIT], F32, name="acc%d_%d_%d" % (u, d, m), tag="bank")
+            acc = psum.tile([P, UNITS[u]], F32, name="acc%d_%d_%d" % (u, d, m), tag="bank")
             mc = slice(m * P, (m + 1) * P)
             nc.tensor.matmul_mx(
                 out=acc[:], lhsT=w_codes[0][:, mc].bitcast(FP8X4), lhsT_scale=w_scales[0][:, mc],
@@ -143,7 +151,9 @@ def tile_mdlstmcellweights_pb_t_kernel(
 
         def sig(u, d, m):
             if (u, d) not in oo:
-                oo[(u, d)] = op.tile([P, MT, UNIT], F32, name="o%d_%d" % (d, u), tag="o%d" % d, bufs=(3 if d == 0 else 2))
+                oo[(u, d)] = op.tile(
+                    [P, MT, UNITS[u]], F32, name="o%d_%d" % (d, u), tag="o%d" % d, bufs=(3 if d == 0 else 2)
+                )
             nc.scalar.activation(
                 out=oo[(u, d)][:, m, :], in_=accs[(u, d, m)][:], func=ACT.Sigmoid, bias=b_sb[:, m:m + 1], scale=1.0
             )
@@ -154,21 +164,24 @@ def tile_mdlstmcellweights_pb_t_kernel(
             for m in range(MT):
                 sig(u, d, m)
 
-        def flat(t, m0, m1):
-            return t[:, m0:m1, :].rearrange("p m n -> p (m n)")
+        def part(t, m0, m1, c0, c1):
+            if c0 == 0 and c1 is None:
+                return t[:, m0:m1, :].rearrange("p m n -> p (m n)")
+            return t[:, m0, c0:c1]
 
-        def prod(u, d, m0=0, m1=MT):
-            of = flat(oo[(u, d)], m0, m1)
+        def prod(u, d, m0=0, m1=MT, c0=0, c1=None):
+            of = part(oo[(u, d)], m0, m1, c0, c1)
             nc.vector.scalar_tensor_tensor(
-                out=of, in0=of, scalar=ws_sb[:, d:d + 1], in1=flat(tt[(u, d)], m0, m1), op0=ALU.mult, op1=ALU.mult
+                out=of, in0=of, scalar=ws_sb[:, d:d + 1], in1=part(tt[(u, d)], m0, m1, c0, c1), op0=ALU.mult, op1=ALU.mult
             )
 
-        def add(u, m0=0, m1=MT):
-            of = flat(oo[(u, 0)], m0, m1)
-            nc.vector.tensor_tensor(out=of, in0=of, in1=flat(oo[(u, 1)], m0, m1), op=ALU.add)
+        def add(u, m0=0, m1=MT, c0=0, c1=None):
+            of = part(oo[(u, 0)], m0, m1, c0, c1)
+            nc.vector.tensor_tensor(out=of, in0=of, in1=part(oo[(u, 1)], m0, m1, c0, c1), op=ALU.add)
 
-        def st(u, m0=0, m1=MT):
-            nc.sync.dma_start(out=out_v[:, m0:m1, u * UNIT:(u + 1) * UNIT], in_=oo[(u, 0)][:, m0:m1, :])
+        def st(u, m0=0, m1=MT, c0=0, c1=None):
+            c1 = UNITS[u] if c1 is None else c1
+            nc.sync.dma_start(out=out_v[:, m0:m1, start[u] + c0:start[u] + c1], in_=oo[(u, 0)][:, m0:m1, c0:c1])
 
         warm = const.tile([P, 1], F32, name="warm")
         nc.vector.memset(warm[:], 0.0)
@@ -187,25 +200,23 @@ def tile_mdlstmcellweights_pb_t_kernel(
             def ldw(wi):
                 nc.sync.dma_start(out=w_raws[wi][:], in_=(w_io, w_ho)[wi].rearrange("(p m) k -> p m k", m=MT))
 
-            ldm(0, 0)
-            ldm(0, 1)
+            def ldsmall():
+                nc.sync.dma_start(out=b_sb[:], in_=b_o.rearrange("(p m) one -> p (m one)", m=MT))
+                nc.sync.dma_start(out=ws_sb[:], in_=weighted_sum.partition_broadcast(P))
+
+            ld("x", 0)
+            ld("h0", 0)
             ldw(0)
             ldw(1)
-            ldc(0, 0)
-            nc.sync.dma_start(out=b_sb[:], in_=b_o.rearrange("(p m) one -> p (m one)", m=MT))
-            nc.sync.dma_start(out=ws_sb[:], in_=weighted_sum.partition_broadcast(P))
-            ldm(0, 2)
-            ldc(0, 1)
-            ldm(1, 0)
-            ldm(1, 1)
-            ldm(1, 2)
-            ldc(1, 0)
-            ldc(1, 1)
-            ldm(2, 0)
-            ldm(2, 1)
-            ldm(2, 2)
-            ldc(2, 0)
-            ldc(2, 1)
+            ld("c0", 0)
+            ldsmall()
+            ld("h1", 0)
+            ld("x", 1)
+            ld("h0", 1)
+            ld("c1", 0)
+            ld("h1", 1)
+            ld("c0", 1)
+            ld("c1", 1)
 
             w_codes = [const.tile([P, MT * P], U32, name="w_codes%d" % wi, align_bytes=64) for wi in range(2)]
             w_scales = [const.tile([P, MT * P], U8, name="w_scales%d" % wi, align_bytes=64) for wi in range(2)]
@@ -219,7 +230,7 @@ def tile_mdlstmcellweights_pb_t_kernel(
                         m = 2 * mp + j
                         for e in range(2):
                             nc.tensor.transpose(wt[:, j, e, :], words[:, m * half + e:(m + 1) * half:2], ident_f[:])
-                    nc.scalar.copy(
+                    (nc.scalar.copy, nc.vector.tensor_copy)[mp](
                         out=w_grps[wi][:].bitcast(F32)[:, mp * 4 * P:(mp + 1) * 4 * P].rearrange("p (j o e) -> p j o e", j=2, e=2),
                         in_=wt[:].rearrange("p j e o -> p j o e"),
                     )
@@ -231,21 +242,23 @@ def tile_mdlstmcellweights_pb_t_kernel(
 
             rgv(0, 0)
             rgv(0, 1)
-            w_turn(0)
             q(0, 0)
+            w_turn(0)
             q(0, 1)
-            w_turn(1)
             wq(0)
+            w_turn(1)
             wq(1)
             rgv(0, 2)
             tanh(0, 0)
             q(0, 2)
+
         op = ctx.enter_context(tc.tile_pool(name="op", bufs=2))
 
         def turn_raw(v):
-            for a in range(3):
-                if (v, a) in BY_TENSOR:
+            if v < N_UNITS:
+                for a in range(3):
                     rgp(v, a)
+                for a in range(3):
                     rgc(v, a)
 
 
@@ -255,41 +268,47 @@ def tile_mdlstmcellweights_pb_t_kernel(
         gates(0, 1)
         tanh(0, 1)
         rgv(1, 0)
+        for nm in names:
+            reload(nm, 0)
+        turn_raw(1)
         for i in range(N_UNITS - 1):
             v = i + 1
-            turn_raw(v)
-            if (v, 1) not in BY_TENSOR:
-                rgv(v, 1)
+            last = v == N_UNITS - 1
+            rgv(v, 1)
             q(v, 0)
             prod(i, 0)
             q(v, 1)
             tanh(v, 0)
             gates(v, 0)
-            prod(i, 1)
             q(v, 2)
-            tanh(v, 1)
-            if v + 1 < N_UNITS:
-                rgv(v + 1, 0)
-            if last_of_chunk(v):
-                for a in range(3):
-                    ldm(chunk_of[v][0] + 2, a)
-            if v + 1 < N_UNITS:
+            prod(i, 1)
+            if last:
+                tanh(v, 1)
                 gates(v, 1)
-                add(i)
-                st(i)
-            if i > 0 and last_of_chunk(i):
-                for d in range(2):
-                    ldc(chunk_of[i][0] + 2, d)
-        g = N_UNITS - 1
+                prod(v, 0, 0, 2)
+            else:
+                tanh(v, 1)
+                turn_raw(v + 1)
+                rgv(v + 1, 0)
+                for nm in ("x", "h0", "h1"):
+                    reload(nm, v)
+                gates(v, 1)
+            add(i)
+            st(i)
+            for nm in ("c0", "c1"):
+                reload(nm, v)
+        v = N_UNITS - 1
+        prod(v, 0, 2, MT)
+        prod(v, 1, 0, 1)
+        prod(v, 1, 1, 2)
         for m in range(MT):
-            mm(g, 1, m)
-            sig(g, 1, m)
-        prod(g, 0, 0, 1)
-        add(g - 1)
-        st(g - 1)
-        for m in range(MT):
-            prod(g, 1, m, m + 1)
-            if m + 1 < MT:
-                prod(g, 0, m + 1, m + 2)
-            add(g, m, m + 1)
-            st(g, m, m + 1)
+            if m < MT - 1:
+                add(v, m, m + 1)
+                st(v, m, m + 1)
+            if m + 2 < MT:
+                prod(v, 1, m + 2, m + 3)
+        half = UNITS[v] // 2
+        m = MT - 1
+        for c in (0, half):
+            add(v, m, m + 1, c, c + half)
+            st(v, m, m + 1, c, c + half)

@@ -98,8 +98,8 @@ def tile_mdlstmcellweights_pb_t_kernel(
             if c0 == c1:
                 return
             nc.vector.tensor_copy(
-                out=grouped(u, a)[:, c0:c1, :].rearrange("p (c i) t -> p c t i", i=4),
-                in_=raw_cols(names[a], u, c0, c1).rearrange("p t (c i) -> p c t i", i=4),
+                out=grouped(u, a)[:, c0:c1, :].rearrange("p (c i) t -> p c t i", i=8),
+                in_=raw_cols(names[a], u, c0, c1).rearrange("p t (c i) -> p c t i", i=8),
             )
 
         def banks(u, a):

@@ -190,6 +190,8 @@ def tile_mdlstmcellweights_pb_t_kernel(
         make_identity(nc, ident_f[:])
         ident = const.tile([P, P], BF16, name="ident")
         nc.vector.tensor_copy(out=ident[:], in_=ident_f[:])
+        zeros = const.tile([P, 3 * P], F32, name="zeros")
+        nc.gpsimd.memset(zeros[:], 0.0)
         b_sb = const.tile([P, MT], BF16, name="b_sb")
         ws_sb = const.tile([P, 2], BF16, name="ws_sb")
 
@@ -240,13 +242,25 @@ def tile_mdlstmcellweights_pb_t_kernel(
                     out=w_codes[wi][:].bitcast(FP8X4), scales=w_scales[wi][:], in_=w_grps[wi][:]
                 )
 
+            def keep_busy(n, nm=None):
+                spare = psum.tile([P, 4 * P], F32, name="spare", tag="bank")
+                if nm is not None:
+                    nc.tensor.matmul(
+                        out=spare[:, 3 * P:4 * P], lhsT=ident[:], rhs=raw_cols(nm, 0, 0, P)[:, 0, :], start=True, stop=True
+                    )
+                nc.tensor.matmul(out=spare[:, 0:n], lhsT=ident_f[:], rhs=zeros[:, 0:n], start=True, stop=True)
+
+            keep_busy(3 * P, "x")
+            keep_busy(2 * P, "h0")
             rgv(0, 0)
             rgv(0, 1)
             q(0, 0)
             w_turn(0)
+            keep_busy(P)
             q(0, 1)
             wq(0)
             w_turn(1)
+            keep_busy(2 * P)
             wq(1)
             rgv(0, 2)
             tanh(0, 0)

@@ -290,8 +290,8 @@ def tile_mdlstmcellweights_pb_t_kernel(
             last = v == N_UNITS - 1
             rgv(v, 1)
             q(v, 0)
-            prod(i, 0)
             q(v, 1)
+            prod(i, 0)
             tanh(v, 0)
             gates(v, 0)
             q(v, 2)

from contextlib import ExitStack

import concourse.mybir as mybir
from concourse.masks import make_identity

FLOPS = 3 * 2 * 512 * 512 * 4096

F32 = mybir.dt.float32
BF16 = mybir.dt.bfloat16
U32 = mybir.dt.uint32
U8 = mybir.dt.uint8
FP8X4 = mybir.dt.float8_e4m3fn_x4
ACT = mybir.ActivationFunctionType
ALU = mybir.AluOpType

P = 128
PACK = 4
CH = 512
MT = CH // P
NPOS = 4096
UNITS = 8 * (512,)
N_UNITS = len(UNITS)
LOADS = (512, 512, 512, 512, 1024, 1024)
def by_tensor(u, a):
    if u == 0:
        return 0
    if u == 1:
        return (0, 0, UNITS[u])[a]
    return (0, 128, UNITS[u])[a]


def tile_mdlstmcellweights_pb_t_kernel(
    tc, x, h_prev_dim0, h_prev_dim1, ct0, ct1, w_io, w_ho, b_o, weighted_sum, out
):
    nc = tc.nc
    with ExitStack() as ctx:
        const = ctx.enter_context(tc.tile_pool(name="const", bufs=1))
        rawp = ctx.enter_context(tc.tile_pool(name="rawp", bufs=2))
        grpp = ctx.enter_context(tc.tile_pool(name="grpp", bufs=2))
        codp = ctx.enter_context(tc.tile_pool(name="codp", bufs=2))
        tp = ctx.enter_context(tc.tile_pool(name="tp", bufs=3))
        psum = ctx.enter_context(tc.psum_pool(name="psum", bufs=8))
        ctx.enter_context(tc.manual_schedule())

        names = ("x", "h0", "h1", "c0", "c1")
        views = {}
        for nm, a in zip(names, (x, h_prev_dim0, h_prev_dim1, ct0, ct1)):
            views[nm] = a.rearrange("(p t) n -> p t n", t=PACK)
        out_v = out.rearrange("(p m) n -> p m n", m=MT)

        start = [sum(UNITS[:u]) for u in range(N_UNITS + 1)]
        where = {}
        last_unit = {}
        first = {}
        for nm in names:
            at = 0
            for c, w in enumerate(LOADS):
                first[(nm, c)] = at
                for u in range(N_UNITS):
                    if at <= start[u] and start[u + 1] <= at + w:
                        where[(nm, u)] = (c, start[u] - at)
                        last_unit[(nm, c)] = u
                at += w

        raw = {}
        grp = {}
        codes = {}
        tt = {}
        oo = {}
        bank_of = {}
        accs = {}

        def ld(nm, c):
            if c >= len(LOADS):
                return
            w = LOADS[c]
            r = rawp.tile([P, PACK, w], BF16, name="raw_%s_%d" % (nm, c), tag="raw_" + nm)
            nc.sync.dma_start(out=r[:], in_=views[nm][:, :, first[(nm, c)]:first[(nm, c)] + w])
            raw[(nm, c)] = r

        def reload(nm, u):
            c = where[(nm, u)][0]
            if last_unit[(nm, c)] == u:
                ld(nm, c + 2)

        def raw_cols(nm, u, c0, c1):
            c, s = where[(nm, u)]
            return raw[(nm, c)][:, :, s + c0:s + c1]

        def grouped(u, a):
            if (u, a) not in grp:
                grp[(u, a)] = grpp.tile([P, UNITS[u], PACK], BF16, name="grp%d_%d" % (a, u), tag="grp%d" % a, align_bytes=64)
            return grp[(u, a)]

        def rgv(u, a, c0=None, c1=None):
            c0 = by_tensor(u, a) if c0 is None else c0
            c1 = UNITS[u] if c1 is None else c1
            if c0 == c1:
                return
            nc.vector.tensor_copy(
                out=grouped(u, a)[:, c0:c1, :].rearrange("p (c i) t -> p c t i", i=8),
                in_=raw_cols(names[a], u, c0, c1).rearrange("p t (c i) -> p c t i", i=8),
            )

        def banks(u, a):
            return [(b0, min(b0 + 2 * P, by_tensor(u, a))) for b0 in range(0, by_tensor(u, a), 2 * P)]

        def rgp(u, a):
            for b0, b1 in banks(u, a):
                bank = psum.tile([P, (b1 - b0) * PACK], BF16, name="rgb%d_%d_%d" % (a, u, b0), tag="bank")
                for n0 in range(b0, b1, P):
                    nc.tensor.matmul(
                        out=bank[:, (n0 - b0) * PACK:(n0 - b0 + P) * PACK].rearrange("p (n t) -> p t n", t=PACK),
                        lhsT=ident[:], rhs=raw_cols(names[a], u, n0, n0 + P), start=True, stop=True,
                    )
                bank_of[(u, a, b0)] = bank

        def rgc(u, a):
            for b0, b1 in banks(u, a):
                nc.scalar.copy(
                    out=grouped(u, a)[:, b0:b1, :].rearrange("p n t -> p (n t)"), in_=bank_of[(u, a, b0)][:]
                )

        def q(u, a):
            w = UNITS[u]
            cd = codp.tile([P, w], U32, name="cod%d_%d" % (a, u), tag="cod%d" % a, align_bytes=64)
            sc = codp.tile([P, w], U8, name="scl%d_%d" % (a, u), tag="scl%d" % a, align_bytes=64)
            nc.vector.quantize_mx(
                out=cd[:].bitcast(FP8X4), scales=sc[:], in_=grp[(u, a)][:].rearrange("p n t -> p (n t)")
            )
            codes[(u, a)] = (cd, sc)

        def tanh(u, d):
            tt[(u, d)] = tp.tile([P, MT, UNITS[u]], F32, name="t%d_%d" % (d, u), tag="t%d" % d)
            nc.scalar.activation(out=tt[(u, d)][:], in_=raw_cols(names[3 + d], u, 0, UNITS[u]), func=ACT.Tanh)

        def mm(u, d, m):
            xc, xs = codes[(u, 0)]
            hc, hs = codes[(u, 1 + d)]
            acc = psum.tile([P, UNITS[u]], F32, name="acc%d_%d_%d" % (u, d, m), tag="bank")
            mc = slice(m * P, (m + 1) * P)
            nc.tensor.matmul_mx(
                out=acc[:], lhsT=w_codes[0][:, mc].bitcast(FP8X4), lhsT_scale=w_scales[0][:, mc],
                rhs=xc[:].bitcast(FP8X4), rhs_scale=xs[:], start=True, stop=False,
            )
            nc.tensor.matmul_mx(
                out=acc[:], lhsT=w_codes[1][:, mc].bitcast(FP8X4), lhsT_scale=w_scales[1][:, mc],
                rhs=hc[:].bitcast(FP8X4), rhs_scale=hs[:], start=False, stop=True,
            )
            accs[(u, d, m)] = acc

        def sig(u, d, m):
            if (u, d) not in oo:
                oo[(u, d)] = op.tile(
                    [P, MT, UNITS[u]], F32, name="o%d_%d" % (d, u), tag="o%d" % d, bufs=(3 if d == 0 else 2)
                )
            nc.scalar.activation(
                out=oo[(u, d)][:, m, :], in_=accs[(u, d, m)][:], func=ACT.Sigmoid, bias=b_sb[:, m:m + 1], scale=1.0
            )

        def gates(u, d):
            for m in range(MT):
                mm(u, d, m)
            for m in range(MT):
                sig(u, d, m)

        def part(t, m0, m1, c0, c1):
            if c0 == 0 and c1 is None:
                return t[:, m0:m1, :].rearrange("p m n -> p (m n)")
            return t[:, m0, c0:c1]

        def prod(u, d, m0=0, m1=MT, c0=0, c1=None):
            of = part(oo[(u, d)], m0, m1, c0, c1)
            nc.vector.scalar_tensor_tensor(
                out=of, in0=of, scalar=ws_sb[:, d:d + 1], in1=part(tt[(u, d)], m0, m1, c0, c1), op0=ALU.mult, op1=ALU.mult
            )

        def add(u, m0=0, m1=MT, c0=0, c1=None):
            of = part(oo[(u, 0)], m0, m1, c0, c1)
            nc.vector.tensor_tensor(out=of, in0=of, in1=part(oo[(u, 1)], m0, m1, c0, c1), op=ALU.add)

        def st(u, m0=0, m1=MT, c0=0, c1=None):
            c1 = UNITS[u] if c1 is None else c1
            nc.sync.dma_start(out=out_v[:, m0:m1, start[u] + c0:start[u] + c1], in_=oo[(u, 0)][:, m0:m1, c0:c1])

        warm = const.tile([P, 1], F32, name="warm")
        nc.vector.memset(warm[:], 0.0)
        nc.scalar.activation(out=warm[:], in_=warm[:], func=ACT.Sigmoid)
        ident_f = const.tile([P, P], F32, name="ident_f")
        make_identity(nc, ident_f[:])
        ident = const.tile([P, P], BF16, name="ident")
        nc.vector.tensor_copy(out=ident[:], in_=ident_f[:])
        zeros = const.tile([P, 3 * P], F32, name="zeros")
        nc.gpsimd.memset(zeros[:], 0.0)
        b_sb = const.tile([P, MT], BF16, name="b_sb")
        ws_sb = const.tile([P, 2], BF16, name="ws_sb")

        with tc.tile_pool(name="wtmp", bufs=1) as wtmp:
            w_raws = [wtmp.tile([P, MT, CH], BF16, name="w_raw%d" % wi) for wi in range(2)]
            w_grps = [wtmp.tile([P, MT * P * PACK], BF16, name="w_grp%d" % wi, align_bytes=64) for wi in range(2)]

            def ldw(wi):
                nc.sync.dma_start(out=w_raws[wi][:], in_=(w_io, w_ho)[wi].rearrange("(p m) k -> p m k", m=MT))

            def ldsmall():
                nc.sync.dma_start(out=b_sb[:], in_=b_o.rearrange("(p m) one -> p (m one)", m=MT))
                nc.sync.dma_start(out=ws_sb[:], in_=weighted_sum.partition_broadcast(P))

            ld("x", 0)
            ld("h0", 0)
            ldw(0)
            ldw(1)
            ld("c0", 0)
            ldsmall()
            ld("h1", 0)
            ld("x", 1)
            ld("h0", 1)
            ld("c1", 0)
            ld("h1", 1)
            ld("c0", 1)
            ld("c1", 1)

            w_codes = [const.tile([P, MT * P], U32, name="w_codes%d" % wi, align_bytes=64) for wi in range(2)]
            w_scales = [const.tile([P, MT * P], U8, name="w_scales%d" % wi, align_bytes=64) for wi in range(2)]

            def w_turn(wi):
                words = w_raws[wi][:].rearrange("p m k -> p (m k)").bitcast(F32)
                half = CH // 2
                for mp in range(2):
                    wt = psum.tile([P, 2, 2, P], F32, name="wt%d_%d" % (wi, mp), tag="bank")
                    for j in range(2):
                        m = 2 * mp + j
                        for e in range(2):
                            nc.tensor.transpose(wt[:, j, e, :], words[:, m * half + e:(m + 1) * half:2], ident_f[:])
                    (nc.scalar.copy, nc.vector.tensor_copy)[mp](
                        out=w_grps[wi][:].bitcast(F32)[:, mp * 4 * P:(mp + 1) * 4 * P].rearrange("p (j o e) -> p j o e", j=2, e=2),
                        in_=wt[:].rearrange("p j e o -> p j o e"),
                    )

            def wq(wi):
                nc.vector.quantize_mx(
                    out=w_codes[wi][:].bitcast(FP8X4), scales=w_scales[wi][:], in_=w_grps[wi][:]
                )

            def keep_busy(n, nm=None):
                spare = psum.tile([P, 4 * P], F32, name="spare", tag="bank")
                if nm is not None:
                    nc.tensor.matmul(
                        out=spare[:, 3 * P:4 * P], lhsT=ident[:], rhs=raw_cols(nm, 0, 0, P)[:, 0, :], start=True, stop=True
                    )
                nc.tensor.matmul(out=spare[:, 0:n], lhsT=ident_f[:], rhs=zeros[:, 0:n], start=True, stop=True)

            keep_busy(3 * P, "x")
            keep_busy(2 * P, "h0")
            rgv(0, 0)
            rgv(0, 1)
            q(0, 0)
            w_turn(0)
            keep_busy(P)
            q(0, 1)
            wq(0)
            w_turn(1)
            keep_busy(2 * P)
            wq(1)
            rgv(0, 2)
            tanh(0, 0)
            q(0, 2)

        op = ctx.enter_context(tc.tile_pool(name="op", bufs=2))

        def turn_raw(v):
            if v < N_UNITS:
                for a in range(3):
                    rgp(v, a)
                for a in range(3):
                    rgc(v, a)


        for m in range(MT):
            mm(0, 0, m)
            sig(0, 0, m)
        gates(0, 1)
        tanh(0, 1)
        rgv(1, 0)
        for nm in names:
            reload(nm, 0)
        turn_raw(1)
        for i in range(N_UNITS - 1):
            v = i + 1
            last = v == N_UNITS - 1
            rgv(v, 1)
            q(v, 0)
            q(v, 1)
            prod(i, 0)
            tanh(v, 0)
            gates(v, 0)
            q(v, 2)
            prod(i, 1)
            if last:
                tanh(v, 1)
                gates(v, 1)
                prod(v, 0, 0, 2)
            else:
                tanh(v, 1)
                turn_raw(v + 1)
                rgv(v + 1, 0)
                for nm in ("x", "h0", "h1"):
                    reload(nm, v)
                gates(v, 1)
            add(i)
            st(i)
            for nm in ("c0", "c1"):
                reload(nm, v)
        v = N_UNITS - 1
        prod(v, 0, 2, MT)
        prod(v, 1, 0, 1)
        prod(v, 1, 1, 2)
        for m in range(MT):
            if m < MT - 1:
                add(v, m, m + 1)
                st(v, m, m + 1)
            if m + 2 < MT:
                prod(v, 1, m + 2, m + 3)
        half = UNITS[v] // 2
        m = MT - 1
        for c in (0, half):
            add(v, m, m + 1, c, c + half)
            st(v, m, m + 1, c, c + half)
